import numpy as np
import ml_dtypes


def mxq(x, axis, fmt="e4m3"):
    dtype, down = {"e4m3": (ml_dtypes.float8_e4m3fn, 7), "e5m2": (ml_dtypes.float8_e5m2, 14)}[fmt]
    v = np.moveaxis(np.asarray(x, np.float32).astype(ml_dtypes.bfloat16).astype(np.float64), axis, -1)
    blocks = v.reshape(v.shape[:-1] + (-1, 32))
    amax = np.abs(blocks).max(-1, keepdims=True)
    byte = np.maximum(np.where(amax > 0, np.frexp(amax)[1] - 1 + 127, 0) - down, 1)
    scale = np.exp2(byte - 127.0)
    codes = (blocks / scale).astype(np.float32).astype(dtype).astype(np.float64)
    return np.moveaxis((codes * scale).reshape(v.shape), -1, axis)


WIDE = False


def mx_kscale(k):
    if not WIDE:
        return np.ones(k)
    levels = np.array([10, -10, 5, -5, 0])
    a = np.random.permutation(np.resize(levels, k // 512 * 4)).reshape(k // 512, 4)
    idx = np.arange(k)
    return np.exp2(a[idx // 512, idx % 128 // 32])


BF16 = ml_dtypes.bfloat16


def bf(x):
    return np.asarray(x, np.float32).astype(BF16)


def f64(x):
    return np.asarray(x).astype(np.float64)


B, N, H, D, C, O = 512, 24, 512, 512, 512, 512
F = D + D + C


def setup_inputs():
    s = mx_kscale(F)
    t = mx_kscale(H)
    ri, rt = mx_kscale(H), mx_kscale(H)
    return {
        "input_text": bf(np.random.standard_normal((B, D)) * s[:D])[:, None, :],
        "input_img": bf(np.random.standard_normal((B, D)) * s[D:D + D])[:, None, :],
        "input_compress": bf(np.random.standard_normal((B, C)) * s[D + D:]),
        "base_text_features": bf(np.random.standard_normal((B, N, H)) * rt),
        "base_img_features": bf(np.random.standard_normal((B, N, H)) * ri),
        "W_user": bf(np.random.standard_normal((H, F)) / np.sqrt(F) / s * t[:, None]),
        "b_user": bf(np.random.standard_normal(H) * 0.3 * t),
        "Wl_img": bf(np.random.standard_normal((O, H)) * 0.5 * np.sqrt(N / H) / ri),
        "bl_img": bf(np.random.standard_normal(O) * 0.2),
        "Wr_img": bf(np.random.standard_normal((O, H)) * 0.5 / np.sqrt(H) / t),
        "Wl_txt": bf(np.random.standard_normal((O, H)) * 0.5 * np.sqrt(N / H) / rt),
        "bl_txt": bf(np.random.standard_normal(O) * 0.2),
        "Wr_txt": bf(np.random.standard_normal((O, H)) * 0.5 / np.sqrt(H) / t),
    }


def reference(input_text, input_img, input_compress, base_text_features, base_img_features,
              W_user, b_user, Wl_img, bl_img, Wr_img, Wl_txt, bl_txt, Wr_txt):
    feat = np.concatenate([f64(input_text)[:, 0], f64(input_img)[:, 0], f64(input_compress)], axis=-1)
    u = (mxq(feat, 1, "e4m3") @ mxq(f64(W_user), 1, "e4m3").T) + f64(b_user)
    mean_img = f64(base_img_features).mean(axis=1)
    mean_txt = f64(base_text_features).mean(axis=1)
    uq = mxq(u, 1, "e4m3")
    out = ((mxq(mean_img, 1, "e4m3") @ mxq(f64(Wl_img), 1, "e4m3").T) + f64(bl_img)
           + (uq @ mxq(f64(Wr_img), 1, "e4m3").T)
           + (mxq(mean_txt, 1, "e4m3") @ mxq(f64(Wl_txt), 1, "e4m3").T) + f64(bl_txt)
           + (uq @ mxq(f64(Wr_txt), 1, "e4m3").T))
    return np.maximum(out, 0.0)

@@ -1,0 +1,267 @@
+from contextlib import ExitStack
+
+import concourse.mybir as mybir
+from concourse.masks import make_identity
+
+BF16 = mybir.dt.bfloat16
+F32 = mybir.dt.float32
+U32 = mybir.dt.uint32
+U8 = mybir.dt.uint8
+FP8X4 = mybir.dt.float8_e4m3fn_x4
+ADD = mybir.AluOpType.add
+IS_GE = mybir.AluOpType.is_ge
+RELU = mybir.ActivationFunctionType.Relu
+
+P = 128
+PACK = 4
+K_PASS = P * PACK
+
+USERS = 512
+NODES = 24
+WIDTH = 512
+FEAT_PASSES = 3
+USER_TILES = USERS // P
+
+GROUP_TILES = 3
+GROUP_USERS = GROUP_TILES * P // NODES
+LOAD_GROUPS = 2
+LOADS_PER_BLOCK = P // (LOAD_GROUPS * GROUP_USERS)
+
+VECTOR_TILES = 3
+NODES_PER_LOAD = 12
+LANES = 4
+
+FLOPS = 2 * USERS * WIDTH * (FEAT_PASSES * K_PASS + 4 * K_PASS) + 2 * USERS * NODES * WIDTH
+
+
+def mx_tiles(pool, name, passes, columns):
+    codes = pool.tile([P, passes, columns], U32, name=name + "_codes", align_bytes=64)
+    scales = pool.tile([P, passes, columns], U8, name=name + "_scales", align_bytes=64)
+    return codes, scales
+
+
+def turn_rows(nc, turn_banks, identity, rows, grouped):
+    turned = turn_banks.tile([P, PACK, P], BF16, name="turned")
+    for t in range(PACK):
+        nc.tensor.transpose(turned[:, t, :], rows[:, t * P : (t + 1) * P], identity)
+    nc.scalar.copy(out=grouped, in_=turned.rearrange("p t r -> p r t"))
+
+
+def quantise(nc, grouped, operand, k_pass, columns):
+    codes, scales = operand
+    nc.vector.quantize_mx(
+        out=codes[:, k_pass, columns].bitcast(FP8X4),
+        scales=scales[:, k_pass, columns],
+        in_=grouped.rearrange("p r t -> p (r t)"),
+    )
+
+
+def quantise_matrix(nc, stage, turn_banks, identity, matrix, operand, k_pass):
+    grouped = stage.tile([P, PACK * P, PACK], BF16, name="grouped", align_bytes=64)
+    for j in range(PACK):
+        turn_rows(nc, turn_banks, identity, matrix[:, j, :], grouped[:, j * P : (j + 1) * P, :])
+    quantise(nc, grouped, operand, k_pass, slice(0, PACK * P))
+
+
+def mx_pass(nc, acc, left, left_pass, left_columns, right, right_pass, right_columns, start, stop):
+    nc.tensor.matmul_mx(
+        out=acc,
+        lhsT=left[0][:, left_pass, left_columns].bitcast(FP8X4),
+        lhsT_scale=left[1][:, left_pass, left_columns],
+        rhs=right[0][:, right_pass, right_columns].bitcast(FP8X4),
+        rhs_scale=right[1][:, right_pass, right_columns],
+        start=start,
+        stop=stop,
+    )
+
+
+def tile_graphlearner_ib_pa_kernel(
+    tc,
+    input_text,
+    input_img,
+    input_compress,
+    base_text_features,
+    base_img_features,
+    W_user,
+    b_user,
+    Wl_img,
+    bl_img,
+    Wr_img,
+    Wl_txt,
+    bl_txt,
+    Wr_txt,
+    out,
+):
+    nc = tc.nc
+    with ExitStack() as ctx:
+        const = ctx.enter_context(tc.tile_pool(name="const", bufs=1))
+        raw = ctx.enter_context(tc.tile_pool(name="raw", bufs=1))
+        keep = ctx.enter_context(tc.tile_pool(name="keep", bufs=1))
+        stage = ctx.enter_context(tc.tile_pool(name="stage", bufs=3))
+        user_rows = ctx.enter_context(tc.tile_pool(name="user_rows", bufs=2))
+        node_rows = ctx.enter_context(tc.tile_pool(name="node_rows", bufs=8))
+        results = ctx.enter_context(tc.tile_pool(name="results", bufs=2))
+        turn_banks = ctx.enter_context(tc.psum_pool(name="turn_banks", bufs=2))
+        sum_banks = ctx.enter_context(tc.psum_pool(name="sum_banks", bufs=2))
+        u_banks = ctx.enter_context(tc.psum_pool(name="u_banks", bufs=2))
+        out_banks = ctx.enter_context(tc.psum_pool(name="out_banks", bufs=2))
+
+        b_user_rows = const.tile([P, P], BF16)
+        nc.vector.memset(b_user_rows, 0.0)
+        nc.sync.dma_start(out=b_user_rows[0:PACK, :], in_=b_user.rearrange("(t p) -> t p", p=P))
+        bias_rows = const.tile([P, WIDTH], BF16)
+        nc.vector.memset(bias_rows, 0.0)
+        nc.sync.dma_start(out=bias_rows[0:1, :], in_=bl_img.rearrange("(o n) -> o n", o=1))
+        nc.sync.dma_start(out=bias_rows[1:2, :], in_=bl_txt.rearrange("(o n) -> o n", o=1))
+
+        w_user_raw = raw.tile([P, PACK, FEAT_PASSES * K_PASS], BF16)
+        nc.sync.dma_start(out=w_user_raw, in_=W_user.rearrange("(j p) k -> p j k", p=P))
+        feat_raw = []
+        for name, part in (
+            ("text_raw", input_text.rearrange("(j p) o k -> p j (o k)", p=P)),
+            ("img_raw", input_img.rearrange("(j p) o k -> p j (o k)", p=P)),
+            ("compress_raw", input_compress.rearrange("(j p) k -> p j k", p=P)),
+        ):
+            part_raw = raw.tile([P, PACK, K_PASS], BF16, name=name)
+            nc.sync.dma_start(out=part_raw, in_=part)
+            feat_raw.append(part_raw)
+        weight_raw = []
+        for name, weight in (("wr_img", Wr_img), ("wr_txt", Wr_txt), ("wl_img", Wl_img), ("wl_txt", Wl_txt)):
+            one_raw = raw.tile([P, PACK, K_PASS], BF16, name=name + "_raw")
+            nc.sync.dma_start(out=one_raw, in_=weight.rearrange("(j p) k -> p j k", p=P))
+            weight_raw.append((name, one_raw))
+
+        identity = const.tile([P, P], BF16)
+        make_identity(nc, identity)
+        ones = const.tile([P, P], BF16)
+        nc.vector.memset(ones, 1.0)
+
+        member_f32 = const.tile([P, GROUP_TILES, GROUP_USERS], F32)
+        nc.gpsimd.memset(member_f32, 1.0)
+        nc.gpsimd.affine_select(
+            out=member_f32,
+            in_=member_f32,
+            pattern=[[P, GROUP_TILES], [-NODES, GROUP_USERS]],
+            compare_op=IS_GE,
+            fill=0.0,
+            base=0,
+            channel_multiplier=1,
+        )
+        nc.gpsimd.affine_select(
+            out=member_f32,
+            in_=member_f32,
+            pattern=[[-P, GROUP_TILES], [NODES, GROUP_USERS]],
+            compare_op=IS_GE,
+            fill=0.0,
+            base=NODES - 1,
+            channel_multiplier=-1,
+        )
+        member = const.tile([P, GROUP_TILES, GROUP_USERS], BF16)
+        nc.vector.tensor_copy(out=member, in_=member_f32)
+
+        b_user_turned = turn_banks.tile([P, P], BF16, name="turned")
+        nc.tensor.transpose(b_user_turned, b_user_rows, identity)
+        b_user_columns = const.tile([P, PACK], F32)
+        nc.vector.tensor_copy(out=b_user_columns, in_=b_user_turned[:, 0:PACK])
+
+        bias_bank = out_banks.tile([P, WIDTH], F32, name="acc")
+        nc.tensor.matmul(out=bias_bank, lhsT=ones, rhs=bias_rows, start=True, stop=True)
+        out_bias = const.tile([P, WIDTH], F32)
+        nc.vector.tensor_copy(out=out_bias, in_=bias_bank)
+
+        w_user_mx = mx_tiles(keep, "w_user", FEAT_PASSES, WIDTH)
+        feat_mx = mx_tiles(keep, "feat", FEAT_PASSES, USERS)
+        for c in range(FEAT_PASSES):
+            k_columns = slice(c * K_PASS, (c + 1) * K_PASS)
+            quantise_matrix(nc, stage, turn_banks, identity, w_user_raw[:, :, k_columns], w_user_mx, c)
+            quantise_matrix(nc, stage, turn_banks, identity, feat_raw[c], feat_mx, c)
+
+        u_mx = mx_tiles(keep, "u", 1, USERS)
+        u_grouped = stage.tile([P, USERS, PACK], BF16, name="grouped", align_bytes=64)
+        for ut in range(USER_TILES):
+            users = slice(ut * P, (ut + 1) * P)
+            u_bank = u_banks.tile([P, PACK, P], F32)
+            for t in range(PACK):
+                for c in range(FEAT_PASSES):
+                    mx_pass(
+                        nc, u_bank[:, t, :], w_user_mx, c, slice(t * P, (t + 1) * P), feat_mx, c, users,
+                        start=(c == 0), stop=(c == FEAT_PASSES - 1),
+                    )
+            nc.vector.tensor_tensor(
+                out=u_grouped[:, users, :],
+                in0=u_bank.rearrange("p t b -> p b t"),
+                in1=b_user_columns.unsqueeze(1).to_broadcast([P, P, PACK]),
+                op=ADD,
+            )
+        quantise(nc, u_grouped, u_mx, 0, slice(0, USERS))
+
+        weight_mx = {}
+        for name, one_raw in weight_raw:
+            weight_mx[name] = mx_tiles(keep, name, 1, WIDTH)
+            quantise_matrix(nc, stage, turn_banks, identity, one_raw, weight_mx[name], 0)
+
+        mean_mx = {"img": mx_tiles(keep, "mean_img", 1, USERS), "txt": mx_tiles(keep, "mean_txt", 1, USERS)}
+        for ut in range(USER_TILES):
+            users = slice(ut * P, (ut + 1) * P)
+            for kind, base in (("img", base_img_features), ("txt", base_text_features)):
+                mean_grouped = stage.tile([P, P, PACK], BF16, name="mean_grouped", align_bytes=64)
+                if kind == "img" and ut < VECTOR_TILES:
+                    nodes = user_rows.tile([P, NODES, WIDTH], BF16)
+                    for first in range(0, NODES, NODES_PER_LOAD):
+                        part = slice(first, first + NODES_PER_LOAD)
+                        nc.sync.dma_start(out=nodes[:, part, :], in_=base[users, part, :])
+                    sums = user_rows.tile([P, LANES, WIDTH], F32)
+                    nc.vector.tensor_tensor(
+                        out=sums, in0=nodes[:, 0:LANES, :], in1=nodes[:, LANES : 2 * LANES, :], op=ADD
+                    )
+                    for first in range(2 * LANES, NODES, LANES):
+                        nc.vector.tensor_tensor(out=sums, in0=sums, in1=nodes[:, first : first + LANES, :], op=ADD)
+                    nc.vector.tensor_tensor(out=sums[:, 0:2, :], in0=sums[:, 0:2, :], in1=sums[:, 2:4, :], op=ADD)
+                    nc.vector.tensor_tensor(out=sums[:, 0, :], in0=sums[:, 0, :], in1=sums[:, 1, :], op=ADD)
+                    mean_rows = user_rows.tile([P, WIDTH], BF16)
+                    nc.scalar.mul(out=mean_rows, in_=sums[:, 0, :], mul=1.0 / NODES)
+                    turn_rows(nc, turn_banks, identity, mean_rows, mean_grouped)
+                else:
+                    all_nodes = base.rearrange("b n h -> (b n) h")
+                    sum_bank = sum_banks.tile([P, PACK, P], F32)
+                    for load in range(LOADS_PER_BLOCK):
+                        tiles = LOAD_GROUPS * GROUP_TILES
+                        first_node = (ut * LOADS_PER_BLOCK + load) * tiles * P
+                        rows = node_rows.tile([P, tiles, WIDTH], BF16)
+                        nc.sync.dma_start(
+                            out=rows,
+                            in_=all_nodes[first_node : first_node + tiles * P, :].rearrange("(i p) h -> p i h", p=P),
+                        )
+                        for g in range(LOAD_GROUPS):
+                            first_user = (load * LOAD_GROUPS + g) * GROUP_USERS
+                            for t in range(PACK):
+                                for r in range(GROUP_TILES):
+                                    low = 0 if r == 0 else r * P // NODES
+                                    high = GROUP_USERS if r == 0 else (r * P + P - 1) // NODES + 1
+                                    nc.tensor.matmul(
+                                        out=sum_bank[:, t, first_user + low : first_user + high],
+                                        lhsT=rows[:, g * GROUP_TILES + r, t * P : (t + 1) * P],
+                                        rhs=member[:, r, low:high],
+                                        start=(r == 0),
+                                        stop=(r == GROUP_TILES - 1),
+                                    )
+                    nc.scalar.mul(out=mean_grouped, in_=sum_bank.rearrange("p t b -> p b t"), mul=1.0 / NODES)
+                quantise(nc, mean_grouped, mean_mx[kind], 0, users)
+
+            acc = out_banks.tile([P, WIDTH], F32)
+            products = (
+                (u_mx, weight_mx["wr_img"]),
+                (u_mx, weight_mx["wr_txt"]),
+                (mean_mx["img"], weight_mx["wl_img"]),
+                (mean_mx["txt"], weight_mx["wl_txt"]),
+            )
+            for i, (left, right) in enumerate(products):
+                mx_pass(
+                    nc, acc, left, 0, users, right, 0, slice(0, WIDTH),
+                    start=(i == 0), stop=(i == len(products) - 1),
+                )
+            biased = results.tile([P, WIDTH], F32)
+            nc.vector.tensor_tensor(out=biased, in0=acc, in1=out_bias, op=ADD)
+            result = results.tile([P, WIDTH], F32)
+            nc.scalar.activation(out=result, in_=biased, func=RELU)
+            nc.scalar.dma_start(out=out[users, :], in_=result)

@@ -22,14 +22,12 @@ WIDTH = 512
 FEAT_PASSES = 3
 USER_TILES = USERS // P
 
-GROUP_TILES = 3
-GROUP_USERS = GROUP_TILES * P // NODES
-LOAD_GROUPS = 2
-LOADS_PER_BLOCK = P // (LOAD_GROUPS * GROUP_USERS)
+LOAD_NODES = 8
+LANES = LOAD_NODES // 2
 
-VECTOR_TILES = 3
-NODES_PER_LOAD = 12
-LANES = 4
+PART_NODES = 3
+SPAN_USERS = P * PART_NODES // NODES
+LOAD_SPANS = 2
 
 FLOPS = 2 * USERS * WIDTH * (FEAT_PASSES * K_PASS + 4 * K_PASS) + 2 * USERS * NODES * WIDTH
 
@@ -38,13 +36,6 @@ def mx_tiles(pool, name, passes, columns):
     codes = pool.tile([P, passes, columns], U32, name=name + "_codes", align_bytes=64)
     scales = pool.tile([P, passes, columns], U8, name=name + "_scales", align_bytes=64)
     return codes, scales
-
-
-def turn_rows(nc, turn_banks, identity, rows, grouped):
-    turned = turn_banks.tile([P, PACK, P], BF16, name="turned")
-    for t in range(PACK):
-        nc.tensor.transpose(turned[:, t, :], rows[:, t * P : (t + 1) * P], identity)
-    nc.scalar.copy(out=grouped, in_=turned.rearrange("p t r -> p r t"))
 
 
 def quantise(nc, grouped, operand, k_pass, columns):
@@ -59,7 +50,11 @@ def quantise(nc, grouped, operand, k_pass, columns):
 def quantise_matrix(nc, stage, turn_banks, identity, matrix, operand, k_pass):
     grouped = stage.tile([P, PACK * P, PACK], BF16, name="grouped", align_bytes=64)
     for j in range(PACK):
-        turn_rows(nc, turn_banks, identity, matrix[:, j, :], grouped[:, j * P : (j + 1) * P, :])
+        turned = turn_banks.tile([P, PACK, P], BF16, name="turned")
+        for t in range(PACK):
+            nc.tensor.transpose(turned[:, t, :], matrix[:, j, t * P : (t + 1) * P], identity)
+        copy = nc.scalar.copy if j % 2 == 0 else nc.vector.tensor_copy
+        copy(out=grouped[:, j * P : (j + 1) * P, :], in_=turned.rearrange("p t r -> p r t"))
     quantise(nc, grouped, operand, k_pass, slice(0, PACK * P))
 
 
@@ -98,12 +93,13 @@ def tile_graphlearner_ib_pa_kernel(
         raw = ctx.enter_context(tc.tile_pool(name="raw", bufs=1))
         keep = ctx.enter_context(tc.tile_pool(name="keep", bufs=1))
         stage = ctx.enter_context(tc.tile_pool(name="stage", bufs=3))
-        user_rows = ctx.enter_context(tc.tile_pool(name="user_rows", bufs=2))
-        node_rows = ctx.enter_context(tc.tile_pool(name="node_rows", bufs=8))
+        user_rows = ctx.enter_context(tc.tile_pool(name="user_rows", bufs=6))
+        pair_sums = ctx.enter_context(tc.tile_pool(name="pair_sums", bufs=4))
+        node_rows = ctx.enter_context(tc.tile_pool(name="node_rows", bufs=6))
         results = ctx.enter_context(tc.tile_pool(name="results", bufs=2))
-        turn_banks = ctx.enter_context(tc.psum_pool(name="turn_banks", bufs=2))
+        turn_banks = ctx.enter_context(tc.psum_pool(name="turn_banks", bufs=3))
         sum_banks = ctx.enter_context(tc.psum_pool(name="sum_banks", bufs=2))
-        u_banks = ctx.enter_context(tc.psum_pool(name="u_banks", bufs=2))
+        u_banks = ctx.enter_context(tc.psum_pool(name="u_banks", bufs=1))
         out_banks = ctx.enter_context(tc.psum_pool(name="out_banks", bufs=2))
 
         b_user_rows = const.tile([P, P], BF16)
@@ -133,30 +129,23 @@ def tile_graphlearner_ib_pa_kernel(
 
         identity = const.tile([P, P], BF16)
         make_identity(nc, identity)
+        identity_f32 = const.tile([P, P], F32)
+        make_identity(nc, identity_f32)
         ones = const.tile([P, P], BF16)
         nc.vector.memset(ones, 1.0)
 
-        member_f32 = const.tile([P, GROUP_TILES, GROUP_USERS], F32)
+        part_users = P // SPAN_USERS
+        member_f32 = const.tile([P, SPAN_USERS], F32)
         nc.gpsimd.memset(member_f32, 1.0)
         nc.gpsimd.affine_select(
-            out=member_f32,
-            in_=member_f32,
-            pattern=[[P, GROUP_TILES], [-NODES, GROUP_USERS]],
-            compare_op=IS_GE,
-            fill=0.0,
-            base=0,
-            channel_multiplier=1,
+            out=member_f32, in_=member_f32, pattern=[[-part_users, SPAN_USERS]],
+            compare_op=IS_GE, fill=0.0, base=0, channel_multiplier=1,
         )
         nc.gpsimd.affine_select(
-            out=member_f32,
-            in_=member_f32,
-            pattern=[[-P, GROUP_TILES], [NODES, GROUP_USERS]],
-            compare_op=IS_GE,
-            fill=0.0,
-            base=NODES - 1,
-            channel_multiplier=-1,
+            out=member_f32, in_=member_f32, pattern=[[part_users, SPAN_USERS]],
+            compare_op=IS_GE, fill=0.0, base=part_users - 1, channel_multiplier=-1,
         )
-        member = const.tile([P, GROUP_TILES, GROUP_USERS], BF16)
+        member = const.tile([P, SPAN_USERS], BF16)
         nc.vector.tensor_copy(out=member, in_=member_f32)
 
         b_user_turned = turn_banks.tile([P, P], BF16, name="turned")
@@ -201,53 +190,53 @@ def tile_graphlearner_ib_pa_kernel(
             quantise_matrix(nc, stage, turn_banks, identity, one_raw, weight_mx[name], 0)
 
         mean_mx = {"img": mx_tiles(keep, "mean_img", 1, USERS), "txt": mx_tiles(keep, "mean_txt", 1, USERS)}
-        for ut in range(USER_TILES):
-            users = slice(ut * P, (ut + 1) * P)
-            for kind, base in (("img", base_img_features), ("txt", base_text_features)):
-                mean_grouped = stage.tile([P, P, PACK], BF16, name="mean_grouped", align_bytes=64)
-                if kind == "img" and ut < VECTOR_TILES:
-                    nodes = user_rows.tile([P, NODES, WIDTH], BF16)
-                    for first in range(0, NODES, NODES_PER_LOAD):
-                        part = slice(first, first + NODES_PER_LOAD)
-                        nc.sync.dma_start(out=nodes[:, part, :], in_=base[users, part, :])
-                    sums = user_rows.tile([P, LANES, WIDTH], F32)
-                    nc.vector.tensor_tensor(
-                        out=sums, in0=nodes[:, 0:LANES, :], in1=nodes[:, LANES : 2 * LANES, :], op=ADD
-                    )
-                    for first in range(2 * LANES, NODES, LANES):
-                        nc.vector.tensor_tensor(out=sums, in0=sums, in1=nodes[:, first : first + LANES, :], op=ADD)
-                    nc.vector.tensor_tensor(out=sums[:, 0:2, :], in0=sums[:, 0:2, :], in1=sums[:, 2:4, :], op=ADD)
-                    nc.vector.tensor_tensor(out=sums[:, 0, :], in0=sums[:, 0, :], in1=sums[:, 1, :], op=ADD)
-                    mean_rows = user_rows.tile([P, WIDTH], BF16)
-                    nc.scalar.mul(out=mean_rows, in_=sums[:, 0, :], mul=1.0 / NODES)
-                    turn_rows(nc, turn_banks, identity, mean_rows, mean_grouped)
-                else:
-                    all_nodes = base.rearrange("b n h -> (b n) h")
-                    sum_bank = sum_banks.tile([P, PACK, P], F32)
-                    for load in range(LOADS_PER_BLOCK):
-                        tiles = LOAD_GROUPS * GROUP_TILES
-                        first_node = (ut * LOADS_PER_BLOCK + load) * tiles * P
-                        rows = node_rows.tile([P, tiles, WIDTH], BF16)
-                        nc.sync.dma_start(
-                            out=rows,
-                            in_=all_nodes[first_node : first_node + tiles * P, :].rearrange("(i p) h -> p i h", p=P),
-                        )
-                        for g in range(LOAD_GROUPS):
-                            first_user = (load * LOAD_GROUPS + g) * GROUP_USERS
-                            for t in range(PACK):
-                                for r in range(GROUP_TILES):
-                                    low = 0 if r == 0 else r * P // NODES
-                                    high = GROUP_USERS if r == 0 else (r * P + P - 1) // NODES + 1
-                                    nc.tensor.matmul(
-                                        out=sum_bank[:, t, first_user + low : first_user + high],
-                                        lhsT=rows[:, g * GROUP_TILES + r, t * P : (t + 1) * P],
-                                        rhs=member[:, r, low:high],
-                                        start=(r == 0),
-                                        stop=(r == GROUP_TILES - 1),
-                                    )
-                    nc.scalar.mul(out=mean_grouped, in_=sum_bank.rearrange("p t b -> p b t"), mul=1.0 / NODES)
-                quantise(nc, mean_grouped, mean_mx[kind], 0, users)
 
+        def load_and_add_users(base, ut, load, sum_bank):
+            loads = NODES // LOAD_NODES
+            nodes = user_rows.tile([P, LOAD_NODES, WIDTH], BF16)
+            nc.sync.dma_start(
+                out=nodes, in_=base[ut * P : (ut + 1) * P, load * LOAD_NODES : (load + 1) * LOAD_NODES, :]
+            )
+            pairs = pair_sums.tile([P, LANES, WIDTH], F32)
+            nc.vector.tensor_tensor(out=pairs, in0=nodes[:, 0:LANES, :], in1=nodes[:, LANES:LOAD_NODES, :], op=ADD)
+            for t in range(PACK):
+                for lane in range(LANES):
+                    nc.tensor.matmul(
+                        out=sum_bank[:, t, :],
+                        lhsT=pairs[:, lane, t * P : (t + 1) * P],
+                        rhs=identity_f32,
+                        is_transpose=True,
+                        start=(load == 0 and t == 0 and lane == 0),
+                        stop=(load == loads - 1 and t == PACK - 1 and lane == LANES - 1),
+                    )
+
+        def load_and_add_nodes(base, ut, load, sum_bank):
+            span_nodes = P * PART_NODES
+            first_node = ut * P * NODES + load * LOAD_SPANS * span_nodes
+            rows = node_rows.tile([P, LOAD_SPANS, PART_NODES, WIDTH], BF16)
+            nc.sync.dma_start(
+                out=rows.rearrange("p s j h -> p s (j h)"),
+                in_=base.rearrange("b n h -> (b n) h")[
+                    first_node : first_node + LOAD_SPANS * span_nodes, :
+                ].rearrange("(s p j) h -> p s (j h)", p=P, j=PART_NODES),
+            )
+            for s in range(LOAD_SPANS):
+                first_user = (load * LOAD_SPANS + s) * SPAN_USERS
+                for t in range(PACK):
+                    for j in range(PART_NODES):
+                        nc.tensor.matmul(
+                            out=sum_bank[:, t, first_user : first_user + SPAN_USERS],
+                            lhsT=rows[:, s, j, t * P : (t + 1) * P],
+                            rhs=member,
+                            start=(j == 0),
+                            stop=(j == PART_NODES - 1),
+                        )
+
+        def finish_block(kind, ut, mean_grouped):
+            users = slice(ut * P, (ut + 1) * P)
+            quantise(nc, mean_grouped, mean_mx[kind], 0, users)
+            if kind == "img":
+                return
             acc = out_banks.tile([P, WIDTH], F32)
             products = (
                 (u_mx, weight_mx["wr_img"]),
@@ -265,3 +254,21 @@ def tile_graphlearner_ib_pa_kernel(
             result = results.tile([P, WIDTH], F32)
             nc.scalar.activation(out=result, in_=biased, func=RELU)
             nc.scalar.dma_start(out=out[users, :], in_=result)
+
+        unfinished = None
+        for ut in range(USER_TILES):
+            for kind, base in (("img", base_img_features), ("txt", base_text_features)):
+                sum_bank = sum_banks.tile([P, PACK, P], F32)
+                by_matmul = kind == "txt" and ut > 0
+                loads = P // (LOAD_SPANS * SPAN_USERS) if by_matmul else NODES // LOAD_NODES
+                for load in range(loads):
+                    if by_matmul:
+                        load_and_add_nodes(base, ut, load, sum_bank)
+                    else:
+                        load_and_add_users(base, ut, load, sum_bank)
+                    if load == 0 and unfinished is not None:
+                        finish_block(*unfinished)
+                mean_grouped = stage.tile([P, P, PACK], BF16, name="mean_grouped", align_bytes=64)
+                nc.scalar.mul(out=mean_grouped, in_=sum_bank.rearrange("p t b -> p b t"), mul=1.0 / NODES)
+                unfinished = (kind, ut, mean_grouped)
+        finish_block(*unfinished)

@@ -53,8 +53,7 @@ def quantise_matrix(nc, stage, turn_banks, identity, matrix, operand, k_pass):
         turned = turn_banks.tile([P, PACK, P], BF16, name="turned")
         for t in range(PACK):
             nc.tensor.transpose(turned[:, t, :], matrix[:, j, t * P : (t + 1) * P], identity)
-        copy = nc.scalar.copy if j % 2 == 0 else nc.vector.tensor_copy
-        copy(out=grouped[:, j * P : (j + 1) * P, :], in_=turned.rearrange("p t r -> p r t"))
+        nc.scalar.copy(out=grouped[:, j * P : (j + 1) * P, :], in_=turned.rearrange("p t r -> p r t"))
     quantise(nc, grouped, operand, k_pass, slice(0, PACK * P))
 
 
@@ -94,7 +93,7 @@ def tile_graphlearner_ib_pa_kernel(
         keep = ctx.enter_context(tc.tile_pool(name="keep", bufs=1))
         stage = ctx.enter_context(tc.tile_pool(name="stage", bufs=3))
         user_rows = ctx.enter_context(tc.tile_pool(name="user_rows", bufs=6))
-        pair_sums = ctx.enter_context(tc.tile_pool(name="pair_sums", bufs=4))
+        running = ctx.enter_context(tc.tile_pool(name="running", bufs=2))
         node_rows = ctx.enter_context(tc.tile_pool(name="node_rows", bufs=6))
         results = ctx.enter_context(tc.tile_pool(name="results", bufs=2))
         turn_banks = ctx.enter_context(tc.psum_pool(name="turn_banks", bufs=3))
@@ -191,26 +190,37 @@ def tile_graphlearner_ib_pa_kernel(
 
         mean_mx = {"img": mx_tiles(keep, "mean_img", 1, USERS), "txt": mx_tiles(keep, "mean_txt", 1, USERS)}
 
-        def load_and_add_users(base, ut, load, sum_bank):
-            loads = NODES // LOAD_NODES
+        def add_users_load(base, ut, load, sums):
             nodes = user_rows.tile([P, LOAD_NODES, WIDTH], BF16)
             nc.sync.dma_start(
                 out=nodes, in_=base[ut * P : (ut + 1) * P, load * LOAD_NODES : (load + 1) * LOAD_NODES, :]
             )
-            pairs = pair_sums.tile([P, LANES, WIDTH], F32)
-            nc.vector.tensor_tensor(out=pairs, in0=nodes[:, 0:LANES, :], in1=nodes[:, LANES:LOAD_NODES, :], op=ADD)
+            if load < 2:
+                nc.vector.tensor_tensor(
+                    out=sums[:, load * LANES : (load + 1) * LANES, :],
+                    in0=nodes[:, 0:LANES, :],
+                    in1=nodes[:, LANES:LOAD_NODES, :],
+                    op=ADD,
+                )
+            else:
+                nc.vector.tensor_tensor(out=sums, in0=sums, in1=nodes, op=ADD)
+
+        def turn_user_sums(sums, sum_bank):
+            nc.vector.tensor_tensor(
+                out=sums[:, 0:LANES, :], in0=sums[:, 0:LANES, :], in1=sums[:, LANES : 2 * LANES, :], op=ADD
+            )
             for t in range(PACK):
                 for lane in range(LANES):
                     nc.tensor.matmul(
                         out=sum_bank[:, t, :],
-                        lhsT=pairs[:, lane, t * P : (t + 1) * P],
+                        lhsT=sums[:, lane, t * P : (t + 1) * P],
                         rhs=identity_f32,
                         is_transpose=True,
-                        start=(load == 0 and t == 0 and lane == 0),
-                        stop=(load == loads - 1 and t == PACK - 1 and lane == LANES - 1),
+                        start=(lane == 0),
+                        stop=(lane == LANES - 1),
                     )
 
-        def load_and_add_nodes(base, ut, load, sum_bank):
+        def add_nodes_load(base, ut, load, sum_bank):
             span_nodes = P * PART_NODES
             first_node = ut * P * NODES + load * LOAD_SPANS * span_nodes
             rows = node_rows.tile([P, LOAD_SPANS, PART_NODES, WIDTH], BF16)
@@ -232,43 +242,62 @@ def tile_graphlearner_ib_pa_kernel(
                             stop=(j == PART_NODES - 1),
                         )
 
-        def finish_block(kind, ut, mean_grouped):
-            users = slice(ut * P, (ut + 1) * P)
-            quantise(nc, mean_grouped, mean_mx[kind], 0, users)
-            if kind == "img":
-                return
-            acc = out_banks.tile([P, WIDTH], F32)
-            products = (
-                (u_mx, weight_mx["wr_img"]),
-                (u_mx, weight_mx["wr_txt"]),
-                (mean_mx["img"], weight_mx["wl_img"]),
-                (mean_mx["txt"], weight_mx["wl_txt"]),
-            )
-            for i, (left, right) in enumerate(products):
-                mx_pass(
-                    nc, acc, left, 0, users, right, 0, slice(0, WIDTH),
-                    start=(i == 0), stop=(i == len(products) - 1),
-                )
-            biased = results.tile([P, WIDTH], F32)
-            nc.vector.tensor_tensor(out=biased, in0=acc, in1=out_bias, op=ADD)
-            result = results.tile([P, WIDTH], F32)
-            nc.scalar.activation(out=result, in_=biased, func=RELU)
-            nc.scalar.dma_start(out=out[users, :], in_=result)
+        def gather(block):
+            if not block["by_matmul"]:
+                block["sum_bank"] = sum_banks.tile([P, PACK, P], F32, name="sum_bank")
+                turn_user_sums(block["sums"], block["sum_bank"])
+            mean_grouped = stage.tile([P, P, PACK], BF16, name="mean_grouped", align_bytes=64)
+            nc.scalar.mul(out=mean_grouped, in_=block["sum_bank"].rearrange("p t b -> p b t"), mul=1.0 / NODES)
+            block["mean_grouped"] = mean_grouped
 
-        unfinished = None
+        def multiply(block):
+            users = slice(block["ut"] * P, (block["ut"] + 1) * P)
+            quantise(nc, block["mean_grouped"], mean_mx[block["kind"]], 0, users)
+            if block["kind"] == "txt":
+                acc = out_banks.tile([P, WIDTH], F32, name="acc")
+                products = (
+                    (u_mx, weight_mx["wr_img"]),
+                    (u_mx, weight_mx["wr_txt"]),
+                    (mean_mx["img"], weight_mx["wl_img"]),
+                    (mean_mx["txt"], weight_mx["wl_txt"]),
+                )
+                for i, (left, right) in enumerate(products):
+                    mx_pass(
+                        nc, acc, left, 0, users, right, 0, slice(0, WIDTH),
+                        start=(i == 0), stop=(i == len(products) - 1),
+                    )
+                block["acc"] = acc
+
+        def store(block):
+            if block["kind"] == "txt":
+                biased = results.tile([P, WIDTH], F32, name="biased")
+                nc.vector.tensor_tensor(out=biased, in0=block["acc"], in1=out_bias, op=ADD)
+                result = results.tile([P, WIDTH], F32, name="result")
+                nc.scalar.activation(out=result, in_=biased, func=RELU)
+                nc.scalar.dma_start(out=out[block["ut"] * P : (block["ut"] + 1) * P, :], in_=result)
+
+        previous = None
         for ut in range(USER_TILES):
             for kind, base in (("img", base_img_features), ("txt", base_text_features)):
-                sum_bank = sum_banks.tile([P, PACK, P], F32)
-                by_matmul = kind == "txt" and ut > 0
-                loads = P // (LOAD_SPANS * SPAN_USERS) if by_matmul else NODES // LOAD_NODES
+                block = {"kind": kind, "ut": ut, "by_matmul": kind == "txt" and ut > 0}
+                if block["by_matmul"]:
+                    block["sum_bank"] = sum_banks.tile([P, PACK, P], F32, name="sum_bank")
+                    loads = P // (LOAD_SPANS * SPAN_USERS)
+                else:
+                    block["sums"] = running.tile([P, 2 * LANES, WIDTH], F32, name="sums")
+                    loads = NODES // LOAD_NODES
                 for load in range(loads):
-                    if by_matmul:
-                        load_and_add_nodes(base, ut, load, sum_bank)
+                    if block["by_matmul"]:
+                        add_nodes_load(base, ut, load, block["sum_bank"])
                     else:
-                        load_and_add_users(base, ut, load, sum_bank)
-                    if load == 0 and unfinished is not None:
-                        finish_block(*unfinished)
-                mean_grouped = stage.tile([P, P, PACK], BF16, name="mean_grouped", align_bytes=64)
-                nc.scalar.mul(out=mean_grouped, in_=sum_bank.rearrange("p t b -> p b t"), mul=1.0 / NODES)
-                unfinished = (kind, ut, mean_grouped)
-        finish_block(*unfinished)
+                        add_users_load(base, ut, load, block["sums"])
+                    if previous is not None and load == 0:
+                        gather(previous)
+                    if previous is not None and load == 1:
+                        multiply(previous)
+                    if previous is not None and load == 2:
+                        store(previous)
+                previous = block
+        gather(previous)
+        multiply(previous)
+        store(previous)

@@ -23,7 +23,9 @@ FEAT_PASSES = 3
 USER_TILES = USERS // P
 
 LOAD_NODES = 8
-LANES = LOAD_NODES // 2
+PAIRS = LOAD_NODES // 2
+USER_LOADS = NODES // LOAD_NODES
+ROW_TILES = 4
 
 PART_NODES = 3
 SPAN_USERS = P * PART_NODES // NODES
@@ -45,16 +47,6 @@ def quantise(nc, grouped, operand, k_pass, columns):
         scales=scales[:, k_pass, columns],
         in_=grouped.rearrange("p r t -> p (r t)"),
     )
-
-
-def quantise_matrix(nc, stage, turn_banks, identity, matrix, operand, k_pass):
-    grouped = stage.tile([P, PACK * P, PACK], BF16, name="grouped", align_bytes=64)
-    for j in range(PACK):
-        turned = turn_banks.tile([P, PACK, P], BF16, name="turned")
-        for t in range(PACK):
-            nc.tensor.transpose(turned[:, t, :], matrix[:, j, t * P : (t + 1) * P], identity)
-        nc.scalar.copy(out=grouped[:, j * P : (j + 1) * P, :], in_=turned.rearrange("p t r -> p r t"))
-    quantise(nc, grouped, operand, k_pass, slice(0, PACK * P))
 
 
 def mx_pass(nc, acc, left, left_pass, left_columns, right, right_pass, right_columns, start, stop):
@@ -89,17 +81,16 @@ def tile_graphlearner_ib_pa_kernel(
     nc = tc.nc
     with ExitStack() as ctx:
         const = ctx.enter_context(tc.tile_pool(name="const", bufs=1))
-        raw = ctx.enter_context(tc.tile_pool(name="raw", bufs=1))
         keep = ctx.enter_context(tc.tile_pool(name="keep", bufs=1))
+        raw = ctx.enter_context(tc.tile_pool(name="raw", bufs=10))
         stage = ctx.enter_context(tc.tile_pool(name="stage", bufs=3))
         user_rows = ctx.enter_context(tc.tile_pool(name="user_rows", bufs=6))
-        running = ctx.enter_context(tc.tile_pool(name="running", bufs=2))
+        pair_sums = ctx.enter_context(tc.tile_pool(name="pair_sums", bufs=4))
         node_rows = ctx.enter_context(tc.tile_pool(name="node_rows", bufs=6))
         results = ctx.enter_context(tc.tile_pool(name="results", bufs=2))
-        turn_banks = ctx.enter_context(tc.psum_pool(name="turn_banks", bufs=3))
+        prep_banks = ctx.enter_context(tc.psum_pool(name="prep_banks", bufs=5))
         sum_banks = ctx.enter_context(tc.psum_pool(name="sum_banks", bufs=2))
-        u_banks = ctx.enter_context(tc.psum_pool(name="u_banks", bufs=1))
-        out_banks = ctx.enter_context(tc.psum_pool(name="out_banks", bufs=2))
+        out_banks = ctx.enter_context(tc.psum_pool(name="out_banks", bufs=1))
 
         b_user_rows = const.tile([P, P], BF16)
         nc.vector.memset(b_user_rows, 0.0)
@@ -109,23 +100,6 @@ def tile_graphlearner_ib_pa_kernel(
         nc.sync.dma_start(out=bias_rows[0:1, :], in_=bl_img.rearrange("(o n) -> o n", o=1))
         nc.sync.dma_start(out=bias_rows[1:2, :], in_=bl_txt.rearrange("(o n) -> o n", o=1))
 
-        w_user_raw = raw.tile([P, PACK, FEAT_PASSES * K_PASS], BF16)
-        nc.sync.dma_start(out=w_user_raw, in_=W_user.rearrange("(j p) k -> p j k", p=P))
-        feat_raw = []
-        for name, part in (
-            ("text_raw", input_text.rearrange("(j p) o k -> p j (o k)", p=P)),
-            ("img_raw", input_img.rearrange("(j p) o k -> p j (o k)", p=P)),
-            ("compress_raw", input_compress.rearrange("(j p) k -> p j k", p=P)),
-        ):
-            part_raw = raw.tile([P, PACK, K_PASS], BF16, name=name)
-            nc.sync.dma_start(out=part_raw, in_=part)
-            feat_raw.append(part_raw)
-        weight_raw = []
-        for name, weight in (("wr_img", Wr_img), ("wr_txt", Wr_txt), ("wl_img", Wl_img), ("wl_txt", Wl_txt)):
-            one_raw = raw.tile([P, PACK, K_PASS], BF16, name=name + "_raw")
-            nc.sync.dma_start(out=one_raw, in_=weight.rearrange("(j p) k -> p j k", p=P))
-            weight_raw.append((name, one_raw))
-
         identity = const.tile([P, P], BF16)
         make_identity(nc, identity)
         identity_f32 = const.tile([P, P], F32)
@@ -133,21 +107,21 @@ def tile_graphlearner_ib_pa_kernel(
         ones = const.tile([P, P], BF16)
         nc.vector.memset(ones, 1.0)
 
-        part_users = P // SPAN_USERS
+        user_parts = P // SPAN_USERS
         member_f32 = const.tile([P, SPAN_USERS], F32)
         nc.gpsimd.memset(member_f32, 1.0)
         nc.gpsimd.affine_select(
-            out=member_f32, in_=member_f32, pattern=[[-part_users, SPAN_USERS]],
+            out=member_f32, in_=member_f32, pattern=[[-user_parts, SPAN_USERS]],
             compare_op=IS_GE, fill=0.0, base=0, channel_multiplier=1,
         )
         nc.gpsimd.affine_select(
-            out=member_f32, in_=member_f32, pattern=[[part_users, SPAN_USERS]],
-            compare_op=IS_GE, fill=0.0, base=part_users - 1, channel_multiplier=-1,
+            out=member_f32, in_=member_f32, pattern=[[user_parts, SPAN_USERS]],
+            compare_op=IS_GE, fill=0.0, base=user_parts - 1, channel_multiplier=-1,
         )
         member = const.tile([P, SPAN_USERS], BF16)
         nc.vector.tensor_copy(out=member, in_=member_f32)
 
-        b_user_turned = turn_banks.tile([P, P], BF16, name="turned")
+        b_user_turned = prep_banks.tile([P, P], BF16, name="prep_bank")
         nc.tensor.transpose(b_user_turned, b_user_rows, identity)
         b_user_columns = const.tile([P, PACK], F32)
         nc.vector.tensor_copy(out=b_user_columns, in_=b_user_turned[:, 0:PACK])
@@ -159,71 +133,84 @@ def tile_graphlearner_ib_pa_kernel(
 
         w_user_mx = mx_tiles(keep, "w_user", FEAT_PASSES, WIDTH)
         feat_mx = mx_tiles(keep, "feat", FEAT_PASSES, USERS)
-        for c in range(FEAT_PASSES):
-            k_columns = slice(c * K_PASS, (c + 1) * K_PASS)
-            quantise_matrix(nc, stage, turn_banks, identity, w_user_raw[:, :, k_columns], w_user_mx, c)
-            quantise_matrix(nc, stage, turn_banks, identity, feat_raw[c], feat_mx, c)
-
         u_mx = mx_tiles(keep, "u", 1, USERS)
-        u_grouped = stage.tile([P, USERS, PACK], BF16, name="grouped", align_bytes=64)
-        for ut in range(USER_TILES):
-            users = slice(ut * P, (ut + 1) * P)
-            u_bank = u_banks.tile([P, PACK, P], F32)
-            for t in range(PACK):
-                for c in range(FEAT_PASSES):
-                    mx_pass(
-                        nc, u_bank[:, t, :], w_user_mx, c, slice(t * P, (t + 1) * P), feat_mx, c, users,
-                        start=(c == 0), stop=(c == FEAT_PASSES - 1),
-                    )
-            nc.vector.tensor_tensor(
-                out=u_grouped[:, users, :],
-                in0=u_bank.rearrange("p t b -> p b t"),
-                in1=b_user_columns.unsqueeze(1).to_broadcast([P, P, PACK]),
-                op=ADD,
-            )
-        quantise(nc, u_grouped, u_mx, 0, slice(0, USERS))
-
-        weight_mx = {}
-        for name, one_raw in weight_raw:
-            weight_mx[name] = mx_tiles(keep, name, 1, WIDTH)
-            quantise_matrix(nc, stage, turn_banks, identity, one_raw, weight_mx[name], 0)
-
+        wr_img_mx = mx_tiles(keep, "wr_img", 1, WIDTH)
+        wr_txt_mx = mx_tiles(keep, "wr_txt", 1, WIDTH)
+        wl_img_mx = mx_tiles(keep, "wl_img", 1, WIDTH)
+        wl_txt_mx = mx_tiles(keep, "wl_txt", 1, WIDTH)
         mean_mx = {"img": mx_tiles(keep, "mean_img", 1, USERS), "txt": mx_tiles(keep, "mean_txt", 1, USERS)}
+        u_grouped = keep.tile([P, USERS, PACK], BF16, align_bytes=64)
 
-        def add_users_load(base, ut, load, sums):
-            nodes = user_rows.tile([P, LOAD_NODES, WIDTH], BF16)
+        feat_parts = (input_text[:, 0, :], input_img[:, 0, :], input_compress)
+        pieces = []
+        for c in range(FEAT_PASSES):
+            pieces.append({"matrix": W_user[:, c * K_PASS : (c + 1) * K_PASS], "operand": w_user_mx, "k_pass": c})
+            pieces.append({"matrix": feat_parts[c], "operand": feat_mx, "k_pass": c})
+        for weight, operand in ((Wr_img, wr_img_mx), (Wr_txt, wr_txt_mx), (Wl_img, wl_img_mx), (Wl_txt, wl_txt_mx)):
+            pieces.append({"matrix": weight, "operand": operand, "k_pass": 0})
+        pieces.append({"user_tiles": (0, 1)})
+        pieces.append({"user_tiles": (2, 3)})
+
+        def begin_piece(piece):
+            if "matrix" in piece:
+                rows = raw.tile([P, ROW_TILES, K_PASS], BF16, name="rows")
+                nc.sync.dma_start(out=rows, in_=piece["matrix"].rearrange("(j p) k -> p j k", p=P))
+                grouped = stage.tile([P, ROW_TILES * P, PACK], BF16, name="grouped", align_bytes=64)
+                for j in range(ROW_TILES):
+                    turned = prep_banks.tile([P, PACK, P], BF16, name="prep_bank")
+                    for t in range(PACK):
+                        nc.tensor.transpose(turned[:, t, :], rows[:, j, t * P : (t + 1) * P], identity)
+                    nc.scalar.copy(out=grouped[:, j * P : (j + 1) * P, :], in_=turned.rearrange("p t r -> p r t"))
+                piece["grouped"] = grouped
+            else:
+                piece["banks"] = []
+                for ut in piece["user_tiles"]:
+                    u_bank = prep_banks.tile([P, PACK, P], F32, name="prep_bank")
+                    for t in range(PACK):
+                        for c in range(FEAT_PASSES):
+                            mx_pass(
+                                nc, u_bank[:, t, :], w_user_mx, c, slice(t * P, (t + 1) * P),
+                                feat_mx, c, slice(ut * P, (ut + 1) * P),
+                                start=(c == 0), stop=(c == FEAT_PASSES - 1),
+                            )
+                    piece["banks"].append(u_bank)
+
+        def end_piece(piece):
+            if "matrix" in piece:
+                quantise(nc, piece["grouped"], piece["operand"], piece["k_pass"], slice(0, ROW_TILES * P))
+            else:
+                for ut, u_bank in zip(piece["user_tiles"], piece["banks"]):
+                    nc.vector.tensor_tensor(
+                        out=u_grouped[:, ut * P : (ut + 1) * P, :],
+                        in0=u_bank.rearrange("p t b -> p b t"),
+                        in1=b_user_columns.unsqueeze(1).to_broadcast([P, P, PACK]),
+                        op=ADD,
+                    )
+                if piece["user_tiles"][-1] == USER_TILES - 1:
+                    quantise(nc, u_grouped, u_mx, 0, slice(0, USERS))
+
+        def add_users_load(base, ut, load, sum_bank):
+            nodes = user_rows.tile([P, LOAD_NODES, WIDTH], BF16, name="nodes")
             nc.sync.dma_start(
                 out=nodes, in_=base[ut * P : (ut + 1) * P, load * LOAD_NODES : (load + 1) * LOAD_NODES, :]
             )
-            if load < 2:
-                nc.vector.tensor_tensor(
-                    out=sums[:, load * LANES : (load + 1) * LANES, :],
-                    in0=nodes[:, 0:LANES, :],
-                    in1=nodes[:, LANES:LOAD_NODES, :],
-                    op=ADD,
-                )
-            else:
-                nc.vector.tensor_tensor(out=sums, in0=sums, in1=nodes, op=ADD)
-
-        def turn_user_sums(sums, sum_bank):
-            nc.vector.tensor_tensor(
-                out=sums[:, 0:LANES, :], in0=sums[:, 0:LANES, :], in1=sums[:, LANES : 2 * LANES, :], op=ADD
-            )
+            pairs = pair_sums.tile([P, PAIRS, WIDTH], F32, name="pairs")
+            nc.vector.tensor_tensor(out=pairs, in0=nodes[:, 0:PAIRS, :], in1=nodes[:, PAIRS:LOAD_NODES, :], op=ADD)
             for t in range(PACK):
-                for lane in range(LANES):
+                for pair in range(PAIRS):
                     nc.tensor.matmul(
                         out=sum_bank[:, t, :],
-                        lhsT=sums[:, lane, t * P : (t + 1) * P],
+                        lhsT=pairs[:, pair, t * P : (t + 1) * P],
                         rhs=identity_f32,
                         is_transpose=True,
-                        start=(lane == 0),
-                        stop=(lane == LANES - 1),
+                        start=(load == 0 and t == 0 and pair == 0),
+                        stop=(load == USER_LOADS - 1 and t == PACK - 1 and pair == PAIRS - 1),
                     )
 
         def add_nodes_load(base, ut, load, sum_bank):
             span_nodes = P * PART_NODES
             first_node = ut * P * NODES + load * LOAD_SPANS * span_nodes
-            rows = node_rows.tile([P, LOAD_SPANS, PART_NODES, WIDTH], BF16)
+            rows = node_rows.tile([P, LOAD_SPANS, PART_NODES, WIDTH], BF16, name="node_rows")
             nc.sync.dma_start(
                 out=rows.rearrange("p s j h -> p s (j h)"),
                 in_=base.rearrange("b n h -> (b n) h")[
@@ -243,9 +230,6 @@ def tile_graphlearner_ib_pa_kernel(
                         )
 
         def gather(block):
-            if not block["by_matmul"]:
-                block["sum_bank"] = sum_banks.tile([P, PACK, P], F32, name="sum_bank")
-                turn_user_sums(block["sums"], block["sum_bank"])
             mean_grouped = stage.tile([P, P, PACK], BF16, name="mean_grouped", align_bytes=64)
             nc.scalar.mul(out=mean_grouped, in_=block["sum_bank"].rearrange("p t b -> p b t"), mul=1.0 / NODES)
             block["mean_grouped"] = mean_grouped
@@ -256,10 +240,10 @@ def tile_graphlearner_ib_pa_kernel(
             if block["kind"] == "txt":
                 acc = out_banks.tile([P, WIDTH], F32, name="acc")
                 products = (
-                    (u_mx, weight_mx["wr_img"]),
-                    (u_mx, weight_mx["wr_txt"]),
-                    (mean_mx["img"], weight_mx["wl_img"]),
-                    (mean_mx["txt"], weight_mx["wl_txt"]),
+                    (u_mx, wr_img_mx),
+                    (u_mx, wr_txt_mx),
+                    (mean_mx["img"], wl_img_mx),
+                    (mean_mx["txt"], wl_txt_mx),
                 )
                 for i, (left, right) in enumerate(products):
                     mx_pass(
@@ -277,20 +261,25 @@ def tile_graphlearner_ib_pa_kernel(
                 nc.scalar.dma_start(out=out[block["ut"] * P : (block["ut"] + 1) * P, :], in_=result)
 
         previous = None
-        for ut in range(USER_TILES):
-            for kind, base in (("img", base_img_features), ("txt", base_text_features)):
-                block = {"kind": kind, "ut": ut, "by_matmul": kind == "txt" and ut > 0}
-                if block["by_matmul"]:
-                    block["sum_bank"] = sum_banks.tile([P, PACK, P], F32, name="sum_bank")
-                    loads = P // (LOAD_SPANS * SPAN_USERS)
-                else:
-                    block["sums"] = running.tile([P, 2 * LANES, WIDTH], F32, name="sums")
-                    loads = NODES // LOAD_NODES
+        begun = None
+        number = 0
+        for kind, base in (("img", base_img_features), ("txt", base_text_features)):
+            for ut in range(USER_TILES):
+                block = {"kind": kind, "ut": ut, "by_matmul": number >= 5}
+                number += 1
+                block["sum_bank"] = sum_banks.tile([P, PACK, P], F32, name="sum_bank")
+                loads = P // (LOAD_SPANS * SPAN_USERS) if block["by_matmul"] else USER_LOADS
                 for load in range(loads):
+                    piece = pieces.pop(0) if pieces else None
+                    if piece is not None:
+                        begin_piece(piece)
                     if block["by_matmul"]:
                         add_nodes_load(base, ut, load, block["sum_bank"])
                     else:
-                        add_users_load(base, ut, load, block["sums"])
+                        add_users_load(base, ut, load, block["sum_bank"])
+                    if begun is not None:
+                        end_piece(begun)
+                    begun = piece
                     if previous is not None and load == 0:
                         gather(previous)
                     if previous is not None and load == 1:

from contextlib import ExitStack

import concourse.mybir as mybir
from concourse.masks import make_identity

BF16 = mybir.dt.bfloat16
F32 = mybir.dt.float32
U32 = mybir.dt.uint32
U8 = mybir.dt.uint8
FP8X4 = mybir.dt.float8_e4m3fn_x4
ADD = mybir.AluOpType.add
IS_GE = mybir.AluOpType.is_ge
RELU = mybir.ActivationFunctionType.Relu

P = 128
PACK = 4
K_PASS = P * PACK

USERS = 512
NODES = 24
WIDTH = 512
FEAT_PASSES = 3
USER_TILES = USERS // P

LOAD_NODES = 8
PAIRS = LOAD_NODES // 2
USER_LOADS = NODES // LOAD_NODES
ROW_TILES = 4

PART_NODES = 3
SPAN_USERS = P * PART_NODES // NODES
LOAD_SPANS = 2

FLOPS = 2 * USERS * WIDTH * (FEAT_PASSES * K_PASS + 4 * K_PASS) + 2 * USERS * NODES * WIDTH


def mx_tiles(pool, name, passes, columns):
    codes = pool.tile([P, passes, columns], U32, name=name + "_codes", align_bytes=64)
    scales = pool.tile([P, passes, columns], U8, name=name + "_scales", align_bytes=64)
    return codes, scales


def quantise(nc, grouped, operand, k_pass, columns):
    codes, scales = operand
    nc.vector.quantize_mx(
        out=codes[:, k_pass, columns].bitcast(FP8X4),
        scales=scales[:, k_pass, columns],
        in_=grouped.rearrange("p r t -> p (r t)"),
    )


def mx_pass(nc, acc, left, left_pass, left_columns, right, right_pass, right_columns, start, stop):
    nc.tensor.matmul_mx(
        out=acc,
        lhsT=left[0][:, left_pass, left_columns].bitcast(FP8X4),
        lhsT_scale=left[1][:, left_pass, left_columns],
        rhs=right[0][:, right_pass, right_columns].bitcast(FP8X4),
        rhs_scale=right[1][:, right_pass, right_columns],
        start=start,
        stop=stop,
    )


def tile_graphlearner_ib_pa_kernel(
    tc,
    input_text,
    input_img,
    input_compress,
    base_text_features,
    base_img_features,
    W_user,
    b_user,
    Wl_img,
    bl_img,
    Wr_img,
    Wl_txt,
    bl_txt,
    Wr_txt,
    out,
):
    nc = tc.nc
    with ExitStack() as ctx:
        const = ctx.enter_context(tc.tile_pool(name="const", bufs=1))
        keep = ctx.enter_context(tc.tile_pool(name="keep", bufs=1))
        raw = ctx.enter_context(tc.tile_pool(name="raw", bufs=10))
        stage = ctx.enter_context(tc.tile_pool(name="stage", bufs=3))
        user_rows = ctx.enter_context(tc.tile_pool(name="user_rows", bufs=6))
        pair_sums = ctx.enter_context(tc.tile_pool(name="pair_sums", bufs=4))
        node_rows = ctx.enter_context(tc.tile_pool(name="node_rows", bufs=6))
        results = ctx.enter_context(tc.tile_pool(name="results", bufs=2))
        prep_banks = ctx.enter_context(tc.psum_pool(name="prep_banks", bufs=5))
        sum_banks = ctx.enter_context(tc.psum_pool(name="sum_banks", bufs=2))
        out_banks = ctx.enter_context(tc.psum_pool(name="out_banks", bufs=1))

        b_user_rows = const.tile([P, P], BF16)
        nc.vector.memset(b_user_rows, 0.0)
        nc.sync.dma_start(out=b_user_rows[0:PACK, :], in_=b_user.rearrange("(t p) -> t p", p=P))
        bias_rows = const.tile([P, WIDTH], BF16)
        nc.vector.memset(bias_rows, 0.0)
        nc.sync.dma_start(out=bias_rows[0:1, :], in_=bl_img.rearrange("(o n) -> o n", o=1))
        nc.sync.dma_start(out=bias_rows[1:2, :], in_=bl_txt.rearrange("(o n) -> o n", o=1))

        identity = const.tile([P, P], BF16)
        make_identity(nc, identity)
        identity_f32 = const.tile([P, P], F32)
        make_identity(nc, identity_f32)
        ones = const.tile([P, P], BF16)
        nc.vector.memset(ones, 1.0)

        user_parts = P // SPAN_USERS
        member_f32 = const.tile([P, SPAN_USERS], F32)
        nc.gpsimd.memset(member_f32, 1.0)
        nc.gpsimd.affine_select(
            out=member_f32, in_=member_f32, pattern=[[-user_parts, SPAN_USERS]],
            compare_op=IS_GE, fill=0.0, base=0, channel_multiplier=1,
        )
        nc.gpsimd.affine_select(
            out=member_f32, in_=member_f32, pattern=[[user_parts, SPAN_USERS]],
            compare_op=IS_GE, fill=0.0, base=user_parts - 1, channel_multiplier=-1,
        )
        member = const.tile([P, SPAN_USERS], BF16)
        nc.vector.tensor_copy(out=member, in_=member_f32)

        b_user_turned = prep_banks.tile([P, P], BF16, name="prep_bank")
        nc.tensor.transpose(b_user_turned, b_user_rows, identity)
        b_user_columns = const.tile([P, PACK], F32)
        nc.vector.tensor_copy(out=b_user_columns, in_=b_user_turned[:, 0:PACK])

        bias_bank = out_banks.tile([P, WIDTH], F32, name="acc")
        nc.tensor.matmul(out=bias_bank, lhsT=ones, rhs=bias_rows, start=True, stop=True)
        out_bias = const.tile([P, WIDTH], F32)
        nc.vector.tensor_copy(out=out_bias, in_=bias_bank)

        w_user_mx = mx_tiles(keep, "w_user", FEAT_PASSES, WIDTH)
        feat_mx = mx_tiles(keep, "feat", FEAT_PASSES, USERS)
        u_mx = mx_tiles(keep, "u", 1, USERS)
        wr_img_mx = mx_tiles(keep, "wr_img", 1, WIDTH)
        wr_txt_mx = mx_tiles(keep, "wr_txt", 1, WIDTH)
        wl_img_mx = mx_tiles(keep, "wl_img", 1, WIDTH)
        wl_txt_mx = mx_tiles(keep, "wl_txt", 1, WIDTH)
        mean_mx = {"img": mx_tiles(keep, "mean_img", 1, USERS), "txt": mx_tiles(keep, "mean_txt", 1, USERS)}
        u_grouped = keep.tile([P, USERS, PACK], BF16, align_bytes=64)

        feat_parts = (input_text[:, 0, :], input_img[:, 0, :], input_compress)
        pieces = []
        for c in range(FEAT_PASSES):
            pieces.append({"matrix": W_user[:, c * K_PASS : (c + 1) * K_PASS], "operand": w_user_mx, "k_pass": c})
            pieces.append({"matrix": feat_parts[c], "operand": feat_mx, "k_pass": c})
        for weight, operand in ((Wr_img, wr_img_mx), (Wr_txt, wr_txt_mx), (Wl_img, wl_img_mx), (Wl_txt, wl_txt_mx)):
            pieces.append({"matrix": weight, "operand": operand, "k_pass": 0})
        pieces.append({"user_tiles": (0, 1)})
        pieces.append({"user_tiles": (2, 3)})

        def begin_piece(piece):
            if "matrix" in piece:
                rows = raw.tile([P, ROW_TILES, K_PASS], BF16, name="rows")
                nc.sync.dma_start(out=rows, in_=piece["matrix"].rearrange("(j p) k -> p j k", p=P))
                grouped = stage.tile([P, ROW_TILES * P, PACK], BF16, name="grouped", align_bytes=64)
                for j in range(ROW_TILES):
                    turned = prep_banks.tile([P, PACK, P], BF16, name="prep_bank")
                    for t in range(PACK):
                        nc.tensor.transpose(turned[:, t, :], rows[:, j, t * P : (t + 1) * P], identity)
                    nc.scalar.copy(out=grouped[:, j * P : (j + 1) * P, :], in_=turned.rearrange("p t r -> p r t"))
                piece["grouped"] = grouped
            else:
                piece["banks"] = []
                for ut in piece["user_tiles"]:
                    u_bank = prep_banks.tile([P, PACK, P], F32, name="prep_bank")
                    for t in range(PACK):
                        for c in range(FEAT_PASSES):
                            mx_pass(
                                nc, u_bank[:, t, :], w_user_mx, c, slice(t * P, (t + 1) * P),
                                feat_mx, c, slice(ut * P, (ut + 1) * P),
                                start=(c == 0), stop=(c == FEAT_PASSES - 1),
                            )
                    piece["banks"].append(u_bank)

        def end_piece(piece):
            if "matrix" in piece:
                quantise(nc, piece["grouped"], piece["operand"], piece["k_pass"], slice(0, ROW_TILES * P))
            else:
                for ut, u_bank in zip(piece["user_tiles"], piece["banks"]):
                    nc.vector.tensor_tensor(
                        out=u_grouped[:, ut * P : (ut + 1) * P, :],
                        in0=u_bank.rearrange("p t b -> p b t"),
                        in1=b_user_columns.unsqueeze(1).to_broadcast([P, P, PACK]),
                        op=ADD,
                    )
                if piece["user_tiles"][-1] == USER_TILES - 1:
                    quantise(nc, u_grouped, u_mx, 0, slice(0, USERS))

        def add_users_load(base, ut, load, sum_bank):
            nodes = user_rows.tile([P, LOAD_NODES, WIDTH], BF16, name="nodes")
            nc.sync.dma_start(
                out=nodes, in_=base[ut * P : (ut + 1) * P, load * LOAD_NODES : (load + 1) * LOAD_NODES, :]
            )
            pairs = pair_sums.tile([P, PAIRS, WIDTH], F32, name="pairs")
            nc.vector.tensor_tensor(out=pairs, in0=nodes[:, 0:PAIRS, :], in1=nodes[:, PAIRS:LOAD_NODES, :], op=ADD)
            for t in range(PACK):
                for pair in range(PAIRS):
                    nc.tensor.matmul(
                        out=sum_bank[:, t, :],
                        lhsT=pairs[:, pair, t * P : (t + 1) * P],
                        rhs=identity_f32,
                        is_transpose=True,
                        start=(load == 0 and t == 0 and pair == 0),
                        stop=(load == USER_LOADS - 1 and t == PACK - 1 and pair == PAIRS - 1),
                    )

        def add_nodes_load(base, ut, load, sum_bank):
            span_nodes = P * PART_NODES
            first_node = ut * P * NODES + load * LOAD_SPANS * span_nodes
            rows = node_rows.tile([P, LOAD_SPANS, PART_NODES, WIDTH], BF16, name="node_rows")
            nc.sync.dma_start(
                out=rows.rearrange("p s j h -> p s (j h)"),
                in_=base.rearrange("b n h -> (b n) h")[
                    first_node : first_node + LOAD_SPANS * span_nodes, :
                ].rearrange("(s p j) h -> p s (j h)", p=P, j=PART_NODES),
            )
            for s in range(LOAD_SPANS):
                first_user = (load * LOAD_SPANS + s) * SPAN_USERS
                for t in range(PACK):
                    for j in range(PART_NODES):
                        nc.tensor.matmul(
                            out=sum_bank[:, t, first_user : first_user + SPAN_USERS],
                            lhsT=rows[:, s, j, t * P : (t + 1) * P],
                            rhs=member,
                            start=(j == 0),
                            stop=(j == PART_NODES - 1),
                        )

        def gather(block):
            mean_grouped = stage.tile([P, P, PACK], BF16, name="mean_grouped", align_bytes=64)
            nc.scalar.mul(out=mean_grouped, in_=block["sum_bank"].rearrange("p t b -> p b t"), mul=1.0 / NODES)
            block["mean_grouped"] = mean_grouped

        def multiply(block):
            users = slice(block["ut"] * P, (block["ut"] + 1) * P)
            quantise(nc, block["mean_grouped"], mean_mx[block["kind"]], 0, users)
            if block["kind"] == "txt":
                acc = out_banks.tile([P, WIDTH], F32, name="acc")
                products = (
                    (u_mx, wr_img_mx),
                    (u_mx, wr_txt_mx),
                    (mean_mx["img"], wl_img_mx),
                    (mean_mx["txt"], wl_txt_mx),
                )
                for i, (left, right) in enumerate(products):
                    mx_pass(
                        nc, acc, left, 0, users, right, 0, slice(0, WIDTH),
                        start=(i == 0), stop=(i == len(products) - 1),
                    )
                block["acc"] = acc

        def store(block):
            if block["kind"] == "txt":
                biased = results.tile([P, WIDTH], F32, name="biased")
                nc.vector.tensor_tensor(out=biased, in0=block["acc"], in1=out_bias, op=ADD)
                result = results.tile([P, WIDTH], F32, name="result")
                nc.scalar.activation(out=result, in_=biased, func=RELU)
                nc.scalar.dma_start(out=out[block["ut"] * P : (block["ut"] + 1) * P, :], in_=result)

        previous = None
        begun = None
        number = 0
        for kind, base in (("img", base_img_features), ("txt", base_text_features)):
            for ut in range(USER_TILES):
                block = {"kind": kind, "ut": ut, "by_matmul": number >= 5}
                number += 1
                block["sum_bank"] = sum_banks.tile([P, PACK, P], F32, name="sum_bank")
                loads = P // (LOAD_SPANS * SPAN_USERS) if block["by_matmul"] else USER_LOADS
                for load in range(loads):
                    piece = pieces.pop(0) if pieces else None
                    if piece is not None:
                        begin_piece(piece)
                    if block["by_matmul"]:
                        add_nodes_load(base, ut, load, block["sum_bank"])
                    else:
                        add_users_load(base, ut, load, block["sum_bank"])
                    if begun is not None:
                        end_piece(begun)
                    begun = piece
                    if previous is not None and load == 0:
                        gather(previous)
                    if previous is not None and load == 1:
                        multiply(previous)
                    if previous is not None and load == 2:
                        store(previous)
                previous = block
        gather(previous)
        multiply(previous)
        store(previous)
